import numpy as np
import ml_dtypes


def mxq(x, axis, fmt="e4m3"):
    dtype, down = {"e4m3": (ml_dtypes.float8_e4m3fn, 7), "e5m2": (ml_dtypes.float8_e5m2, 14)}[fmt]
    v = np.moveaxis(np.asarray(x, np.float32).astype(ml_dtypes.bfloat16).astype(np.float64), axis, -1)
    blocks = v.reshape(v.shape[:-1] + (-1, 32))
    amax = np.abs(blocks).max(-1, keepdims=True)
    byte = np.maximum(np.where(amax > 0, np.frexp(amax)[1] - 1 + 127, 0) - down, 1)
    scale = np.exp2(byte - 127.0)
    codes = (blocks / scale).astype(np.float32).astype(dtype).astype(np.float64)
    return np.moveaxis((codes * scale).reshape(v.shape), -1, axis)


WIDE = False


def mx_kscale(k):
    if not WIDE:
        return np.ones(k)
    levels = np.array([10, -10, 5, -5, 0])
    if k % 512:
        return np.exp2(np.random.permutation(np.resize(levels, k // 32))).repeat(32)
    a = np.empty((k // 512, 16))
    for p in range(k // 512):
        a[p, :8] = np.random.permutation(np.resize(levels, 8))
        for g in range(8):
            far = levels[np.abs(levels - a[p, g]) >= 10]
            a[p, g + 8] = far[np.random.randint(len(far))]
    return np.exp2(a.ravel()).repeat(32)


BF16 = ml_dtypes.bfloat16


def bf(x):
    return np.asarray(x, np.float32).astype(BF16)


def f64(x):
    return np.asarray(x).astype(np.float64)


B, IN_F, OUT_F = 10240, 1024, 256
EPS = 1e-5


def setup_inputs():
    s = mx_kscale(IN_F)
    scale = 1.0 / np.sqrt(IN_F)
    return {"x": bf(np.random.standard_normal((B, IN_F)) * s),
            "y": bf(np.random.standard_normal((B, OUT_F))),
            "weight": bf(np.random.uniform(-scale, scale, (OUT_F, IN_F)) / s[None, :]),
            "bias": bf(np.random.uniform(-0.5, 0.5, OUT_F)),
            "running_mean": bf(np.random.standard_normal(OUT_F) * 0.3),
            "running_var": bf(np.random.uniform(0.5, 1.5, OUT_F)),
            "norm_weight": bf(1.0 + 0.1 * np.random.standard_normal(OUT_F)),
            "norm_bias": bf(np.random.standard_normal(OUT_F) * 0.3)}


def reference(x, y, weight, bias, running_mean, running_var, norm_weight, norm_bias):
    linear = (mxq(f64(x), 1, "e4m3") @ mxq(f64(weight), 1, "e4m3").T) + f64(bias)
    inv_std = 1.0 / np.sqrt(f64(running_var) + EPS)
    norm = (linear - f64(running_mean)) * inv_std * f64(norm_weight) + f64(norm_bias)
    return (norm + f64(y)) * f64(y)

@@ -1,0 +1,239 @@
+from contextlib import ExitStack
+
+import concourse.mybir as mybir
+from concourse.masks import make_identity
+
+F32 = mybir.dt.float32
+BF16 = mybir.dt.bfloat16
+U32 = mybir.dt.uint32
+U8 = mybir.dt.uint8
+FP8X4 = mybir.dt.float8_e4m3fn_x4
+ACT = mybir.ActivationFunctionType
+ALU = mybir.AluOpType
+
+P = 128
+B, IN_F, OUT_F = 10240, 1024, 256
+EPS = 1e-5
+FLOPS = 2 * B * IN_F * OUT_F
+
+CH = 512
+NCH = B // CH
+JG = 8
+NG = B // (P * JG)
+MANUAL = True
+
+
+def tile_modelnew_t_kernel(
+    tc, x, y, weight, bias, running_mean, running_var, norm_weight, norm_bias, out
+):
+    nc = tc.nc
+    xv = x.rearrange("(g p j) k -> g p (j k)", p=P, j=JG)
+    yv = y.rearrange("(g p j) f -> g p (j f)", p=P, j=JG)
+    ov = out.rearrange("(g p j) f -> g p (j f)", p=P, j=JG)
+
+    with ExitStack() as ctx:
+        if MANUAL:
+            ctx.enter_context(tc.manual_schedule())
+        const = ctx.enter_context(tc.tile_pool(name="const", bufs=1))
+        xin = ctx.enter_context(tc.tile_pool(name="xin", bufs=4))
+        yin = ctx.enter_context(tc.tile_pool(name="yin", bufs=6))
+        work = ctx.enter_context(tc.tile_pool(name="work", bufs=3))
+        outp = ctx.enter_context(tc.tile_pool(name="outp", bufs=10))
+        xtp = ctx.enter_context(tc.psum_pool(name="xtp", bufs=4))
+        linp = ctx.enter_context(tc.psum_pool(name="linp", bufs=2))
+        nbp = ctx.enter_context(tc.psum_pool(name="nbp", bufs=2))
+
+        xs = {}
+        ys = {}
+        grps = {}
+        cods = {}
+        scls = {}
+        lins = {}
+        nts = {}
+        nbs = {}
+        outs = {}
+
+        def load_x(g, pieces):
+            xt = xin.tile([P, JG * IN_F], BF16, name="xs", tag="xs")
+            w = JG * IN_F // pieces
+            for s in range(pieces):
+                nc.sync.dma_start(out=xt[:, s * w:(s + 1) * w], in_=xv[g][:, s * w:(s + 1) * w])
+            xs[g] = xt
+
+        def load_y(g):
+            yt = yin.tile([P, JG * OUT_F], BF16, name="ys", tag="ys")
+            nc.sync.dma_start(out=yt[:], in_=yv[g])
+            ys[g] = yt
+
+        ident = const.tile([P, P], F32, name="ident")
+        make_identity(nc, ident[:])
+        vrows = const.tile([P, P], BF16, name="vrows")
+        nc.vector.memset(vrows[:], 0.0)
+        warm = const.tile([P, 1], F32, name="warm")
+        nc.vector.memset(warm[:], 1.0)
+        for v, vec in enumerate((bias, running_mean, running_var, norm_weight, norm_bias)):
+            nc.scalar.dma_start(out=vrows[2 * v:2 * v + 2, :], in_=vec.rearrange("(h p) -> h p", h=2))
+        warm2 = const.tile([P, 1], F32, name="warm2")
+        nc.scalar.sqrt(warm2[:], warm[:])
+
+        w_sb = const.tile([P, 2 * IN_F], BF16, name="w_sb")
+        nc.sync.dma_start(
+            out=w_sb[:].rearrange("p (h k) -> p h k", h=2),
+            in_=weight.rearrange("(h p) k -> p h k", p=P),
+        )
+        load_x(0, 4)
+        load_x(1, 2)
+        load_y(0)
+        load_x(2, 1)
+        load_y(1)
+        load_x(3, 1)
+        load_y(2)
+
+        w32 = w_sb[:].bitcast(F32).rearrange("p (h w) -> p h w", h=2)
+        wgrp = const.tile([P, 2048], BF16, name="wgrp", align_bytes=64)
+        wgrp32 = wgrp[:].bitcast(F32).rearrange("p (g c u) -> p g c u", g=2, u=2)
+        for g in range(2):
+            wt = xtp.tile([P, 2, 256], F32, name="wt", tag="xt")
+            for u in range(2):
+                for h in range(2):
+                    nc.tensor.transpose(wt[:, u, h * P:(h + 1) * P], w32[:, h, 256 * g + u:256 * (g + 1):2], ident[:])
+            nc.scalar.copy(out=wgrp32[:, g], in_=wt[:].rearrange("p u c -> p c u"))
+        wcod = const.tile([P, 512], U32, name="wcod", align_bytes=64)
+        wscl = const.tile([P, 512], U8, name="wscl", align_bytes=64)
+        nc.vector.quantize_mx(out=wcod[:].bitcast(FP8X4), scales=wscl[:], in_=wgrp[:])
+
+        def x_bank(i, b):
+            g, jp = b // 2, b % 2
+            if b == 0:
+                grps[i] = work.tile([P, 4096], BF16, name="grp", tag="grp", align_bytes=64)
+            x32 = xs[i // 2][:].bitcast(F32).rearrange("p (j w) -> p j w", j=JG)
+            grp32 = grps[i][:].bitcast(F32).rearrange("p (g c u) -> p g c u", g=2, u=2)
+            bank = xtp.tile([P, 2, 256], F32, name="xt", tag="xt")
+            for u in range(2):
+                for jj in range(2):
+                    j = (i % 2) * 4 + jp * 2 + jj
+                    nc.tensor.transpose(bank[:, u, jj * P:(jj + 1) * P], x32[:, j, 256 * g + u:256 * (g + 1):2], ident[:])
+            nc.scalar.copy(
+                out=grp32[:, g, jp * 256:(jp + 1) * 256, :],
+                in_=bank[:].rearrange("p u c -> p c u"),
+            )
+
+        def stage_q(i, g):
+            if g == 0:
+                cods[i] = work.tile([P, 1024], U32, name="cod", tag="cod", align_bytes=64)
+                scls[i] = work.tile([P, 1024], U8, name="scl", tag="scl", align_bytes=64)
+            nc.vector.quantize_mx(
+                out=cods[i][:, g * CH:(g + 1) * CH].bitcast(FP8X4),
+                scales=scls[i][:, g * CH:(g + 1) * CH],
+                in_=grps[i][:, g * 2048:(g + 1) * 2048],
+            )
+
+        def stage_m(i, h):
+            lin = linp.tile([P, CH], F32, name="lin", tag="lin")
+            for g in range(2):
+                w0 = g * 256 + h * P
+                nc.tensor.matmul_mx(
+                    out=lin[:],
+                    lhsT=wcod[:, w0:w0 + P].bitcast(FP8X4),
+                    lhsT_scale=wscl[:, w0:w0 + P],
+                    rhs=cods[i][:, g * CH:(g + 1) * CH].bitcast(FP8X4),
+                    rhs_scale=scls[i][:, g * CH:(g + 1) * CH],
+                    start=(g == 0),
+                    stop=(g == 1),
+                )
+            lins[(i, h)] = lin
+
+        def stage_a(i):
+            nt = work.tile([P, 2, CH], F32, name="nt", tag="nt")
+            for h in range(2):
+                nc.scalar.activation(
+                    out=nt[:, h, :], in_=lins[(i, h)][:], func=ACT.Identity,
+                    scale=s_col[:, h:h + 1], bias=t_col[:, h:h + 1],
+                )
+            nts[i] = nt
+
+        def stage_b(i):
+            nbs[i] = []
+            for jp in range(2):
+                nb = nbp.tile([P, 2, 256], F32, name="nb", tag="nb")
+                for jj in range(2):
+                    for h in range(2):
+                        c0 = (jp * 2 + jj) * P
+                        nc.tensor.transpose(nb[:, jj, h * P:(h + 1) * P], nts[i][:, h, c0:c0 + P], ident[:])
+                nbs[i].append(nb)
+
+        def stage_d(i, jp):
+            if jp == 0:
+                outs[i] = outp.tile([P, 4 * OUT_F], F32, name="o", tag="o")
+            o3 = outs[i][:].rearrange("p (j f) -> p j f", j=4)
+            y3 = ys[i // 2][:].rearrange("p (j f) -> p j f", j=JG)
+            j0 = (i % 2) * 4 + jp * 2
+            nc.vector.tensor_tensor(
+                out=o3[:, jp * 2:jp * 2 + 2, :], in0=nbs[i][jp][:], in1=y3[:, j0:j0 + 2, :], op=ALU.add
+            )
+
+        def stage_u(i, lo, n):
+            o = outs[i]
+            c0 = (i % 2) * 4 * OUT_F + lo
+            nc.vector.tensor_tensor(
+                out=o[:, lo:lo + n], in0=o[:, lo:lo + n], in1=ys[i // 2][:, c0:c0 + n], op=ALU.mult
+            )
+
+        def stage_st(i, lo, n):
+            c0 = (i % 2) * 4 * OUT_F + lo
+            nc.sync.dma_start(out=ov[i // 2][:, c0:c0 + n], in_=outs[i][:, lo:lo + n])
+
+        vrows32 = const.tile([P, P], F32, name="vrows32")
+        nc.vector.tensor_copy(out=vrows32[:], in_=vrows[:])
+        pv = nbp.tile([P, 2, 256], F32, name="pv", tag="nb")
+        nc.tensor.transpose(pv[:, 0, 0:P], vrows32[:], ident[:])
+        prm = const.tile([P, 10], F32, name="prm")
+        nc.vector.tensor_copy(out=prm[:], in_=pv[:, 0, 0:10])
+        tmp = const.tile([P, 8], F32, name="tmp")
+        s_col = const.tile([P, 2], F32, name="s_col")
+        t_col = const.tile([P, 2], F32, name="t_col")
+        nc.vector.tensor_scalar_add(out=tmp[:, 0:2], in0=prm[:, 4:6], scalar1=EPS)
+        sd = const.tile([P, 2], F32, name="sd")
+        nc.scalar.sqrt(sd[:], tmp[:, 0:2])
+        nc.vector.reciprocal(out=tmp[:, 2:4], in_=sd[:])
+        nc.vector.tensor_tensor(out=s_col[:], in0=tmp[:, 2:4], in1=prm[:, 6:8], op=ALU.mult)
+        nc.vector.tensor_tensor(out=tmp[:, 4:6], in0=prm[:, 0:2], in1=prm[:, 2:4], op=ALU.subtract)
+        nc.vector.tensor_tensor(out=tmp[:, 6:8], in0=tmp[:, 4:6], in1=s_col[:], op=ALU.mult)
+        nc.vector.tensor_tensor(out=t_col[:], in0=tmp[:, 6:8], in1=prm[:, 8:10], op=ALU.add)
+
+        for b in range(4):
+            x_bank(0, b)
+        stage_q(0, 0)
+        stage_q(0, 1)
+        for k in range(NCH + 1):
+            nxt = k + 1 < NCH
+            if nxt:
+                for b in range(4):
+                    x_bank(k + 1, b)
+                g_new = (k + 1) // 2 + 4
+                if (k + 1) % 2 == 1 and g_new < NG:
+                    load_x(g_new, 1)
+                    load_y(g_new - 1)
+                    if g_new == NG - 1:
+                        load_y(g_new)
+            if k < NCH:
+                stage_m(k, 0)
+                stage_m(k, 1)
+                stage_a(k)
+            if nxt:
+                stage_q(k + 1, 0)
+                stage_q(k + 1, 1)
+            if k >= 1:
+                stage_b(k - 1)
+                if k - 1 == NCH - 1:
+                    stage_d(k - 1, 0)
+                    stage_d(k - 1, 1)
+                    for jp in range(2):
+                        stage_u(k - 1, jp * 512, 512)
+                        stage_st(k - 1, jp * 512, 512)
+                else:
+                    stage_d(k - 1, 0)
+                    stage_d(k - 1, 1)
+                    stage_u(k - 1, 0, 512)
+                    stage_u(k - 1, 512, 512)
+                    stage_st(k - 1, 0, 1024)

@@ -20,7 +20,7 @@ CH = 512
 NCH = B // CH
 JG = 8
 NG = B // (P * JG)
-MANUAL = True
+XB = 4
 
 
 def tile_modelnew_t_kernel(
@@ -32,19 +32,19 @@ def tile_modelnew_t_kernel(
     ov = out.rearrange("(g p j) f -> g p (j f)", p=P, j=JG)
 
     with ExitStack() as ctx:
-        if MANUAL:
-            ctx.enter_context(tc.manual_schedule())
+        ctx.enter_context(tc.manual_schedule())
         const = ctx.enter_context(tc.tile_pool(name="const", bufs=1))
-        xin = ctx.enter_context(tc.tile_pool(name="xin", bufs=4))
+        xin = ctx.enter_context(tc.tile_pool(name="xin", bufs=XB))
         yin = ctx.enter_context(tc.tile_pool(name="yin", bufs=6))
         work = ctx.enter_context(tc.tile_pool(name="work", bufs=3))
-        outp = ctx.enter_context(tc.tile_pool(name="outp", bufs=10))
+        outp = ctx.enter_context(tc.tile_pool(name="outp", bufs=8))
         xtp = ctx.enter_context(tc.psum_pool(name="xtp", bufs=4))
         linp = ctx.enter_context(tc.psum_pool(name="linp", bufs=2))
         nbp = ctx.enter_context(tc.psum_pool(name="nbp", bufs=2))
 
         xs = {}
         ys = {}
+        xrs = {}
         grps = {}
         cods = {}
         scls = {}
@@ -67,6 +67,8 @@ def tile_modelnew_t_kernel(
 
         ident = const.tile([P, P], F32, name="ident")
         make_identity(nc, ident[:])
+        identb = const.tile([P, P], BF16, name="identb")
+        make_identity(nc, identb[:])
         vrows = const.tile([P, P], BF16, name="vrows")
         nc.vector.memset(vrows[:], 0.0)
         warm = const.tile([P, 1], F32, name="warm")
@@ -102,17 +104,26 @@ def tile_modelnew_t_kernel(
         wscl = const.tile([P, 512], U8, name="wscl", align_bytes=64)
         nc.vector.quantize_mx(out=wcod[:].bitcast(FP8X4), scales=wscl[:], in_=wgrp[:])
 
+        def stage_r(i):
+            xr = work.tile([P, 4 * IN_F], BF16, name="xr", tag="xr")
+            x32 = xs[i // 2][:].bitcast(F32)[:, (i % 2) * 2048:(i % 2 + 1) * 2048]
+            nc.vector.tensor_copy(
+                out=xr[:].bitcast(F32).rearrange("p (n u w) -> p n u w", n=8, u=2),
+                in_=x32.rearrange("p (n w u) -> p n u w", n=8, u=2),
+            )
+            xrs[i] = xr
+
         def x_bank(i, b):
             g, jp = b // 2, b % 2
             if b == 0:
                 grps[i] = work.tile([P, 4096], BF16, name="grp", tag="grp", align_bytes=64)
-            x32 = xs[i // 2][:].bitcast(F32).rearrange("p (j w) -> p j w", j=JG)
+            x32 = xrs[i][:].bitcast(F32).rearrange("p (j w) -> p j w", j=4)
             grp32 = grps[i][:].bitcast(F32).rearrange("p (g c u) -> p g c u", g=2, u=2)
             bank = xtp.tile([P, 2, 256], F32, name="xt", tag="xt")
             for u in range(2):
                 for jj in range(2):
-                    j = (i % 2) * 4 + jp * 2 + jj
-                    nc.tensor.transpose(bank[:, u, jj * P:(jj + 1) * P], x32[:, j, 256 * g + u:256 * (g + 1):2], ident[:])
+                    c0 = 256 * g + 128 * u
+                    nc.tensor.transpose(bank[:, u, jj * P:(jj + 1) * P], x32[:, jp * 2 + jj, c0:c0 + P], ident[:])
             nc.scalar.copy(
                 out=grp32[:, g, jp * 256:(jp + 1) * 256, :],
                 in_=bank[:].rearrange("p u c -> p c u"),
@@ -152,32 +163,49 @@ def tile_modelnew_t_kernel(
                 )
             nts[i] = nt
 
-        def stage_b(i):
-            nbs[i] = []
-            for jp in range(2):
-                nb = nbp.tile([P, 2, 256], F32, name="nb", tag="nb")
-                for jj in range(2):
-                    for h in range(2):
-                        c0 = (jp * 2 + jj) * P
-                        nc.tensor.transpose(nb[:, jj, h * P:(h + 1) * P], nts[i][:, h, c0:c0 + P], ident[:])
-                nbs[i].append(nb)
+        def y_on_pe(i, jp):
+            return not (jp == 1 and i % 2 == 1)
 
-        def stage_d(i, jp):
+        def stage_b(i, jp):
+            nb = nbp.tile([P, 2, 256], F32, name="nb", tag="nb")
+            add_y = y_on_pe(i, jp)
+            if add_y:
+                c0 = ((i % 2) * 4 + jp * 2) * OUT_F
+                nc.tensor.matmul(
+                    out=nb[:].rearrange("p j f -> p (j f)"), lhsT=identb[:], rhs=ys[i // 2][:, c0:c0 + 512],
+                    start=True, stop=False,
+                )
+            for jj in range(2):
+                for h in range(2):
+                    c0 = (jp * 2 + jj) * P
+                    nc.tensor.matmul(
+                        out=nb[:, jj, h * P:(h + 1) * P], lhsT=nts[i][:, h, c0:c0 + P], rhs=ident[:],
+                        start=not add_y, stop=(not add_y) or (jj == 1 and h == 1), is_transpose=True,
+                    )
+            nbs[(i, jp)] = nb
+
+        def y_cols(i, jp):
+            c0 = ((i % 2) * 4 + jp * 2) * OUT_F
+            return ys[i // 2][:, c0:c0 + 512]
+
+        def o_cols(i, jp):
             if jp == 0:
                 outs[i] = outp.tile([P, 4 * OUT_F], F32, name="o", tag="o")
-            o3 = outs[i][:].rearrange("p (j f) -> p j f", j=4)
-            y3 = ys[i // 2][:].rearrange("p (j f) -> p j f", j=JG)
-            j0 = (i % 2) * 4 + jp * 2
+            return outs[i][:, jp * 512:(jp + 1) * 512]
+
+        def stage_d(i, jp):
             nc.vector.tensor_tensor(
-                out=o3[:, jp * 2:jp * 2 + 2, :], in0=nbs[i][jp][:], in1=y3[:, j0:j0 + 2, :], op=ALU.add
+                out=o_cols(i, jp), in0=nbs[(i, jp)][:].rearrange("p j f -> p (j f)"), in1=y_cols(i, jp), op=ALU.add
             )
 
-        def stage_u(i, lo, n):
-            o = outs[i]
-            c0 = (i % 2) * 4 * OUT_F + lo
-            nc.vector.tensor_tensor(
-                out=o[:, lo:lo + n], in0=o[:, lo:lo + n], in1=ys[i // 2][:, c0:c0 + n], op=ALU.mult
-            )
+        def stage_u(i, jp):
+            if y_on_pe(i, jp):
+                nc.vector.tensor_tensor(
+                    out=o_cols(i, jp), in0=nbs[(i, jp)][:].rearrange("p j f -> p (j f)"), in1=y_cols(i, jp), op=ALU.mult
+                )
+            else:
+                o = outs[i][:, jp * 512:(jp + 1) * 512]
+                nc.vector.tensor_tensor(out=o, in0=o, in1=y_cols(i, jp), op=ALU.mult)
 
         def stage_st(i, lo, n):
             c0 = (i % 2) * 4 * OUT_F + lo
@@ -201,39 +229,49 @@ def tile_modelnew_t_kernel(
         nc.vector.tensor_tensor(out=tmp[:, 6:8], in0=tmp[:, 4:6], in1=s_col[:], op=ALU.mult)
         nc.vector.tensor_tensor(out=t_col[:], in0=tmp[:, 6:8], in1=prm[:, 8:10], op=ALU.add)
 
+        stage_r(0)
         for b in range(4):
             x_bank(0, b)
+        stage_r(1)
+        load_x(XB, 1)
+        load_y(XB - 1)
         stage_q(0, 0)
         stage_q(0, 1)
         for k in range(NCH + 1):
             nxt = k + 1 < NCH
-            if nxt:
-                for b in range(4):
-                    x_bank(k + 1, b)
-                g_new = (k + 1) // 2 + 4
-                if (k + 1) % 2 == 1 and g_new < NG:
+            prv = k >= 1
+            if k + 2 < NCH:
+                stage_r(k + 2)
+                g_new = (k + 2) // 2 + XB
+                if (k + 2) % 2 == 1 and g_new < NG:
                     load_x(g_new, 1)
                     load_y(g_new - 1)
                     if g_new == NG - 1:
                         load_y(g_new)
+            if nxt:
+                x_bank(k + 1, 0)
+                x_bank(k + 1, 1)
+            if prv:
+                stage_b(k - 1, 0)
+                stage_u(k - 1, 0)
+            if nxt:
+                x_bank(k + 1, 2)
+                x_bank(k + 1, 3)
+                stage_q(k + 1, 0)
+            if prv:
+                stage_b(k - 1, 1)
+                if not y_on_pe(k - 1, 1):
+                    stage_d(k - 1, 1)
             if k < NCH:
                 stage_m(k, 0)
                 stage_m(k, 1)
                 stage_a(k)
             if nxt:
-                stage_q(k + 1, 0)
                 stage_q(k + 1, 1)
-            if k >= 1:
-                stage_b(k - 1)
-                if k - 1 == NCH - 1:
-                    stage_d(k - 1, 0)
-                    stage_d(k - 1, 1)
-                    for jp in range(2):
-                        stage_u(k - 1, jp * 512, 512)
-                        stage_st(k - 1, jp * 512, 512)
+            if prv:
+                stage_u(k - 1, 1)
+                if k == NCH:
+                    stage_st(k - 1, 0, 512)
+                    stage_st(k - 1, 512, 512)
                 else:
-                    stage_d(k - 1, 0)
-                    stage_d(k - 1, 1)
-                    stage_u(k - 1, 0, 512)
-                    stage_u(k - 1, 512, 512)
                     stage_st(k - 1, 0, 1024)

@@ -16,11 +16,13 @@ B, IN_F, OUT_F = 10240, 1024, 256
 EPS = 1e-5
 FLOPS = 2 * B * IN_F * OUT_F
 
-CH = 512
-NCH = B // CH
 JG = 8
 NG = B // (P * JG)
-XB = 4
+JU = 2
+CU = JU * P
+UG = JG // JU
+NU = B // CU
+XB = 5
 
 
 def tile_modelnew_t_kernel(
@@ -53,44 +55,148 @@ def tile_modelnew_t_kernel(
         nbs = {}
         outs = {}
 
-        def load_x(g, pieces):
-            xt = xin.tile([P, JG * IN_F], BF16, name="xs", tag="xs")
-            w = JG * IN_F // pieces
-            for s in range(pieces):
-                nc.sync.dma_start(out=xt[:, s * w:(s + 1) * w], in_=xv[g][:, s * w:(s + 1) * w])
-            xs[g] = xt
+        def load_x(g, lo, hi):
+            if lo == 0:
+                xs[g] = xin.tile([P, JG * IN_F], BF16, name="xs", tag="xs")
+            w = JU * IN_F
+            nc.sync.dma_start(out=xs[g][:, lo * w:hi * w], in_=xv[g][:, lo * w:hi * w])
 
         def load_y(g):
             yt = yin.tile([P, JG * OUT_F], BF16, name="ys", tag="ys")
             nc.sync.dma_start(out=yt[:], in_=yv[g])
             ys[g] = yt
 
-        ident = const.tile([P, P], F32, name="ident")
-        make_identity(nc, ident[:])
-        identb = const.tile([P, P], BF16, name="identb")
-        make_identity(nc, identb[:])
-        vrows = const.tile([P, P], BF16, name="vrows")
-        nc.vector.memset(vrows[:], 0.0)
-        warm = const.tile([P, 1], F32, name="warm")
-        nc.vector.memset(warm[:], 1.0)
-        for v, vec in enumerate((bias, running_mean, running_var, norm_weight, norm_bias)):
-            nc.scalar.dma_start(out=vrows[2 * v:2 * v + 2, :], in_=vec.rearrange("(h p) -> h p", h=2))
-        warm2 = const.tile([P, 1], F32, name="warm2")
-        nc.scalar.sqrt(warm2[:], warm[:])
-
+        load_x(0, 0, 1)
+        load_x(0, 1, 2)
         w_sb = const.tile([P, 2 * IN_F], BF16, name="w_sb")
         nc.sync.dma_start(
             out=w_sb[:].rearrange("p (h k) -> p h k", h=2),
             in_=weight.rearrange("(h p) k -> p h k", p=P),
         )
-        load_x(0, 4)
-        load_x(1, 2)
+        load_x(0, 2, 4)
         load_y(0)
-        load_x(2, 1)
+        load_x(1, 0, 4)
         load_y(1)
-        load_x(3, 1)
+        load_x(2, 0, 4)
         load_y(2)
+        load_x(3, 0, 4)
+        load_y(3)
+        load_x(4, 0, 4)
 
+        ident = const.tile([P, P], F32, name="ident")
+        make_identity(nc, ident[:])
+        vrows = const.tile([P, P], BF16, name="vrows")
+        nc.gpsimd.memset(vrows[:], 0.0)
+        for v, vec in enumerate((bias, running_mean, running_var, norm_weight, norm_bias)):
+            nc.scalar.dma_start(out=vrows[2 * v:2 * v + 2, :], in_=vec.rearrange("(h p) -> h p", h=2))
+        identb = const.tile([P, P], BF16, name="identb")
+        make_identity(nc, identb[:])
+        half = const.tile([P, 2], F32, name="half")
+        nc.gpsimd.memset(half[:], -0.5)
+        vrows32 = const.tile([P, P], F32, name="vrows32")
+        nc.gpsimd.tensor_copy(out=vrows32[:], in_=vrows[:])
+
+        def stage_r(i):
+            xr = work.tile([P, JU * IN_F], BF16, name="xr", tag="xr")
+            w = JU * IN_F // 2
+            q = i % UG
+            x32 = xs[i // UG][:].bitcast(F32)[:, q * w:(q + 1) * w]
+            nc.vector.tensor_copy(
+                out=xr[:].bitcast(F32).rearrange("p (n u w) -> p n u w", n=2 * JU, u=2),
+                in_=x32.rearrange("p (n w u) -> p n u w", n=2 * JU, u=2),
+            )
+            xrs[i] = xr
+
+        def stage_x(i):
+            grps[i] = work.tile([P, 2 * CU * 4], BF16, name="grp", tag="grp", align_bytes=64)
+            x32 = xrs[i][:].bitcast(F32).rearrange("p (j w) -> p j w", j=JU)
+            grp32 = grps[i][:].bitcast(F32).rearrange("p (g c u) -> p g c u", g=2, u=2)
+            for g in range(2):
+                bank = xtp.tile([P, 2, CU], F32, name="xt", tag="xt")
+                for u in range(2):
+                    for jj in range(JU):
+                        c0 = 256 * g + 128 * u
+                        nc.tensor.transpose(bank[:, u, jj * P:(jj + 1) * P], x32[:, jj, c0:c0 + P], ident[:])
+                nc.scalar.copy(out=grp32[:, g], in_=bank[:].rearrange("p u c -> p c u"))
+
+        def stage_q(i):
+            cods[i] = work.tile([P, 2 * CU], U32, name="cod", tag="cod", align_bytes=64)
+            scls[i] = work.tile([P, 2 * CU], U8, name="scl", tag="scl", align_bytes=64)
+            nc.vector.quantize_mx(out=cods[i][:].bitcast(FP8X4), scales=scls[i][:], in_=grps[i][:])
+
+        def stage_m(i):
+            lin = linp.tile([P, 2, CU], F32, name="lin", tag="lin")
+            for h in range(2):
+                for g in range(2):
+                    w0 = g * 256 + h * P
+                    nc.tensor.matmul_mx(
+                        out=lin[:, h, :],
+                        lhsT=wcod[:, w0:w0 + P].bitcast(FP8X4),
+                        lhsT_scale=wscl[:, w0:w0 + P],
+                        rhs=cods[i][:, g * CU:(g + 1) * CU].bitcast(FP8X4),
+                        rhs_scale=scls[i][:, g * CU:(g + 1) * CU],
+                        start=(g == 0),
+                        stop=(g == 1),
+                    )
+            lins[i] = lin
+
+        def stage_a(i):
+            nt = work.tile([P, 2, CU], F32, name="nt", tag="nt")
+            for h in range(2):
+                nc.scalar.activation(
+                    out=nt[:, h, :], in_=lins[i][:, h, :], func=ACT.Identity,
+                    scale=s_col[:, h:h + 1], bias=t_col[:, h:h + 1],
+                )
+            nts[i] = nt
+
+        def y_cols(i):
+            q = i % UG
+            return ys[i // UG][:, q * JU * OUT_F:(q + 1) * JU * OUT_F]
+
+        def y_on_pe(i):
+            return i % 4 != 1
+
+        def stage_y(i):
+            nb = nbp.tile([P, JU * OUT_F], F32, name="nb", tag="nb")
+            if y_on_pe(i):
+                nc.tensor.matmul(out=nb[:], lhsT=identb[:], rhs=y_cols(i), start=True, stop=False)
+            nbs[i] = nb
+
+        def stage_b(i):
+            add_y = y_on_pe(i)
+            for jj in range(JU):
+                for h in range(2):
+                    c0 = jj * OUT_F + h * P
+                    nc.tensor.matmul(
+                        out=nbs[i][:, c0:c0 + P], lhsT=nts[i][:, h, jj * P:(jj + 1) * P], rhs=ident[:],
+                        start=not add_y, stop=(not add_y) or (jj == 1 and h == 1), is_transpose=True,
+                    )
+
+        def o_cols(i):
+            if i % 2 == 0:
+                outs[i // 2] = outp.tile([P, 2 * JU * OUT_F], F32, name="o", tag="o")
+            w = JU * OUT_F
+            return outs[i // 2][:, (i % 2) * w:(i % 2 + 1) * w]
+
+        def stage_u(i):
+            op = ALU.mult if y_on_pe(i) else ALU.add
+            nc.vector.tensor_tensor(out=o_cols(i), in0=nbs[i][:], in1=y_cols(i), op=op)
+
+        def stage_u2(i):
+            w = JU * OUT_F
+            o = outs[i // 2][:, (i % 2) * w:(i % 2 + 1) * w]
+            nc.vector.tensor_tensor(out=o, in0=o, in1=y_cols(i), op=ALU.mult)
+
+        def stage_st(i, n):
+            w = JU * OUT_F
+            nc.sync.dma_start(
+                out=ov[i // UG][:, (i % UG) * w:(i % UG + n) * w],
+                in_=outs[i // 2][:, (i % 2) * w:(i % 2 + n) * w],
+            )
+
+        stage_r(0)
+        stage_r(1)
+        stage_x(0)
         w32 = w_sb[:].bitcast(F32).rearrange("p (h w) -> p h w", h=2)
         wgrp = const.tile([P, 2048], BF16, name="wgrp", align_bytes=64)
         wgrp32 = wgrp[:].bitcast(F32).rearrange("p (g c u) -> p g c u", g=2, u=2)
@@ -100,178 +206,48 @@ def tile_modelnew_t_kernel(
                 for h in range(2):
                     nc.tensor.transpose(wt[:, u, h * P:(h + 1) * P], w32[:, h, 256 * g + u:256 * (g + 1):2], ident[:])
             nc.scalar.copy(out=wgrp32[:, g], in_=wt[:].rearrange("p u c -> p c u"))
+        stage_q(0)
         wcod = const.tile([P, 512], U32, name="wcod", align_bytes=64)
         wscl = const.tile([P, 512], U8, name="wscl", align_bytes=64)
         nc.vector.quantize_mx(out=wcod[:].bitcast(FP8X4), scales=wscl[:], in_=wgrp[:])
 
-        def stage_r(i):
-            xr = work.tile([P, 4 * IN_F], BF16, name="xr", tag="xr")
-            x32 = xs[i // 2][:].bitcast(F32)[:, (i % 2) * 2048:(i % 2 + 1) * 2048]
-            nc.vector.tensor_copy(
-                out=xr[:].bitcast(F32).rearrange("p (n u w) -> p n u w", n=8, u=2),
-                in_=x32.rearrange("p (n w u) -> p n u w", n=8, u=2),
-            )
-            xrs[i] = xr
-
-        def x_bank(i, b):
-            g, jp = b // 2, b % 2
-            if b == 0:
-                grps[i] = work.tile([P, 4096], BF16, name="grp", tag="grp", align_bytes=64)
-            x32 = xrs[i][:].bitcast(F32).rearrange("p (j w) -> p j w", j=4)
-            grp32 = grps[i][:].bitcast(F32).rearrange("p (g c u) -> p g c u", g=2, u=2)
-            bank = xtp.tile([P, 2, 256], F32, name="xt", tag="xt")
-            for u in range(2):
-                for jj in range(2):
-                    c0 = 256 * g + 128 * u
-                    nc.tensor.transpose(bank[:, u, jj * P:(jj + 1) * P], x32[:, jp * 2 + jj, c0:c0 + P], ident[:])
-            nc.scalar.copy(
-                out=grp32[:, g, jp * 256:(jp + 1) * 256, :],
-                in_=bank[:].rearrange("p u c -> p c u"),
-            )
-
-        def stage_q(i, g):
-            if g == 0:
-                cods[i] = work.tile([P, 1024], U32, name="cod", tag="cod", align_bytes=64)
-                scls[i] = work.tile([P, 1024], U8, name="scl", tag="scl", align_bytes=64)
-            nc.vector.quantize_mx(
-                out=cods[i][:, g * CH:(g + 1) * CH].bitcast(FP8X4),
-                scales=scls[i][:, g * CH:(g + 1) * CH],
-                in_=grps[i][:, g * 2048:(g + 1) * 2048],
-            )
-
-        def stage_m(i, h):
-            lin = linp.tile([P, CH], F32, name="lin", tag="lin")
-            for g in range(2):
-                w0 = g * 256 + h * P
-                nc.tensor.matmul_mx(
-                    out=lin[:],
-                    lhsT=wcod[:, w0:w0 + P].bitcast(FP8X4),
-                    lhsT_scale=wscl[:, w0:w0 + P],
-                    rhs=cods[i][:, g * CH:(g + 1) * CH].bitcast(FP8X4),
-                    rhs_scale=scls[i][:, g * CH:(g + 1) * CH],
-                    start=(g == 0),
-                    stop=(g == 1),
-                )
-            lins[(i, h)] = lin
-
-        def stage_a(i):
-            nt = work.tile([P, 2, CH], F32, name="nt", tag="nt")
-            for h in range(2):
-                nc.scalar.activation(
-                    out=nt[:, h, :], in_=lins[(i, h)][:], func=ACT.Identity,
-                    scale=s_col[:, h:h + 1], bias=t_col[:, h:h + 1],
-                )
-            nts[i] = nt
-
-        def y_on_pe(i, jp):
-            return not (jp == 1 and i % 2 == 1)
-
-        def stage_b(i, jp):
-            nb = nbp.tile([P, 2, 256], F32, name="nb", tag="nb")
-            add_y = y_on_pe(i, jp)
-            if add_y:
-                c0 = ((i % 2) * 4 + jp * 2) * OUT_F
-                nc.tensor.matmul(
-                    out=nb[:].rearrange("p j f -> p (j f)"), lhsT=identb[:], rhs=ys[i // 2][:, c0:c0 + 512],
-                    start=True, stop=False,
-                )
-            for jj in range(2):
-                for h in range(2):
-                    c0 = (jp * 2 + jj) * P
-                    nc.tensor.matmul(
-                        out=nb[:, jj, h * P:(h + 1) * P], lhsT=nts[i][:, h, c0:c0 + P], rhs=ident[:],
-                        start=not add_y, stop=(not add_y) or (jj == 1 and h == 1), is_transpose=True,
-                    )
-            nbs[(i, jp)] = nb
-
-        def y_cols(i, jp):
-            c0 = ((i % 2) * 4 + jp * 2) * OUT_F
-            return ys[i // 2][:, c0:c0 + 512]
-
-        def o_cols(i, jp):
-            if jp == 0:
-                outs[i] = outp.tile([P, 4 * OUT_F], F32, name="o", tag="o")
-            return outs[i][:, jp * 512:(jp + 1) * 512]
-
-        def stage_d(i, jp):
-            nc.vector.tensor_tensor(
-                out=o_cols(i, jp), in0=nbs[(i, jp)][:].rearrange("p j f -> p (j f)"), in1=y_cols(i, jp), op=ALU.add
-            )
-
-        def stage_u(i, jp):
-            if y_on_pe(i, jp):
-                nc.vector.tensor_tensor(
-                    out=o_cols(i, jp), in0=nbs[(i, jp)][:].rearrange("p j f -> p (j f)"), in1=y_cols(i, jp), op=ALU.mult
-                )
-            else:
-                o = outs[i][:, jp * 512:(jp + 1) * 512]
-                nc.vector.tensor_tensor(out=o, in0=o, in1=y_cols(i, jp), op=ALU.mult)
-
-        def stage_st(i, lo, n):
-            c0 = (i % 2) * 4 * OUT_F + lo
-            nc.sync.dma_start(out=ov[i // 2][:, c0:c0 + n], in_=outs[i][:, lo:lo + n])
-
-        vrows32 = const.tile([P, P], F32, name="vrows32")
-        nc.vector.tensor_copy(out=vrows32[:], in_=vrows[:])
-        pv = nbp.tile([P, 2, 256], F32, name="pv", tag="nb")
-        nc.tensor.transpose(pv[:, 0, 0:P], vrows32[:], ident[:])
+        pv = nbp.tile([P, P], F32, name="pv", tag="nb")
+        nc.tensor.transpose(pv[:], vrows32[:], ident[:])
         prm = const.tile([P, 10], F32, name="prm")
-        nc.vector.tensor_copy(out=prm[:], in_=pv[:, 0, 0:10])
+        nc.scalar.copy(out=prm[:], in_=pv[:, 0:10])
         tmp = const.tile([P, 8], F32, name="tmp")
         s_col = const.tile([P, 2], F32, name="s_col")
         t_col = const.tile([P, 2], F32, name="t_col")
-        nc.vector.tensor_scalar_add(out=tmp[:, 0:2], in0=prm[:, 4:6], scalar1=EPS)
-        sd = const.tile([P, 2], F32, name="sd")
-        nc.scalar.sqrt(sd[:], tmp[:, 0:2])
-        nc.vector.reciprocal(out=tmp[:, 2:4], in_=sd[:])
-        nc.vector.tensor_tensor(out=s_col[:], in0=tmp[:, 2:4], in1=prm[:, 6:8], op=ALU.mult)
-        nc.vector.tensor_tensor(out=tmp[:, 4:6], in0=prm[:, 0:2], in1=prm[:, 2:4], op=ALU.subtract)
-        nc.vector.tensor_tensor(out=tmp[:, 6:8], in0=tmp[:, 4:6], in1=s_col[:], op=ALU.mult)
-        nc.vector.tensor_tensor(out=t_col[:], in0=tmp[:, 6:8], in1=prm[:, 8:10], op=ALU.add)
+        nc.gpsimd.tensor_scalar(out=tmp[:, 0:2], in0=prm[:, 4:6], scalar1=EPS, scalar2=None, op0=ALU.add)
+        nc.gpsimd.tensor_tensor(out=tmp[:, 2:4], in0=tmp[:, 0:2], in1=half[:], op=ALU.pow)
+        nc.gpsimd.tensor_tensor(out=s_col[:], in0=tmp[:, 2:4], in1=prm[:, 6:8], op=ALU.mult)
+        nc.gpsimd.tensor_tensor(out=tmp[:, 4:6], in0=prm[:, 0:2], in1=prm[:, 2:4], op=ALU.subtract)
+        nc.gpsimd.tensor_tensor(out=tmp[:, 6:8], in0=tmp[:, 4:6], in1=s_col[:], op=ALU.mult)
+        nc.gpsimd.tensor_tensor(out=t_col[:], in0=tmp[:, 6:8], in1=prm[:, 8:10], op=ALU.add)
 
-        stage_r(0)
-        for b in range(4):
-            x_bank(0, b)
-        stage_r(1)
-        load_x(XB, 1)
-        load_y(XB - 1)
-        stage_q(0, 0)
-        stage_q(0, 1)
-        for k in range(NCH + 1):
-            nxt = k + 1 < NCH
-            prv = k >= 1
-            if k + 2 < NCH:
+        for k in range(NU + 2):
+            if 1 <= k < NU:
+                stage_q(k)
+            if k >= 2 and not y_on_pe(k - 2):
+                stage_u2(k - 2)
+            if k >= 2 and k - 2 >= NU - 2:
+                stage_st(k - 2, 1)
+            elif k >= 2 and k % 2 == 1:
+                stage_st(k - 3, 2)
+            if k + 2 < NU:
                 stage_r(k + 2)
-                g_new = (k + 2) // 2 + XB
-                if (k + 2) % 2 == 1 and g_new < NG:
-                    load_x(g_new, 1)
+                g_new = (k + 2) // UG + XB
+                if (k + 2) % UG == UG - 1 and g_new < NG:
+                    load_x(g_new, 0, 4)
                     load_y(g_new - 1)
                     if g_new == NG - 1:
                         load_y(g_new)
-            if nxt:
-                x_bank(k + 1, 0)
-                x_bank(k + 1, 1)
-            if prv:
-                stage_b(k - 1, 0)
-                stage_u(k - 1, 0)
-            if nxt:
-                x_bank(k + 1, 2)
-                x_bank(k + 1, 3)
-                stage_q(k + 1, 0)
-            if prv:
-                stage_b(k - 1, 1)
-                if not y_on_pe(k - 1, 1):
-                    stage_d(k - 1, 1)
-            if k < NCH:
-                stage_m(k, 0)
-                stage_m(k, 1)
+            if k + 1 < NU:
+                stage_x(k + 1)
+            if 1 <= k <= NU:
+                stage_b(k - 1)
+                stage_u(k - 1)
+            if k < NU:
+                stage_m(k)
+                stage_y(k)
                 stage_a(k)
-            if nxt:
-                stage_q(k + 1, 1)
-            if prv:
-                stage_u(k - 1, 1)
-                if k == NCH:
-                    stage_st(k - 1, 0, 512)
-                    stage_st(k - 1, 512, 512)
-                else:
-                    stage_st(k - 1, 0, 1024)

@@ -38,7 +38,7 @@ def tile_modelnew_t_kernel(
         const = ctx.enter_context(tc.tile_pool(name="const", bufs=1))
         xin = ctx.enter_context(tc.tile_pool(name="xin", bufs=XB))
         yin = ctx.enter_context(tc.tile_pool(name="yin", bufs=6))
-        work = ctx.enter_context(tc.tile_pool(name="work", bufs=3))
+        work = ctx.enter_context(tc.tile_pool(name="work", bufs=4))
         outp = ctx.enter_context(tc.tile_pool(name="outp", bufs=8))
         xtp = ctx.enter_context(tc.psum_pool(name="xtp", bufs=4))
         linp = ctx.enter_context(tc.psum_pool(name="linp", bufs=2))
@@ -66,6 +66,10 @@ def tile_modelnew_t_kernel(
             nc.sync.dma_start(out=yt[:], in_=yv[g])
             ys[g] = yt
 
+        vrows = const.tile([P, P], BF16, name="vrows")
+        nc.vector.memset(vrows[:], 0.0)
+        for v, vec in enumerate((bias, running_mean, running_var, norm_weight, norm_bias)):
+            nc.scalar.dma_start(out=vrows[2 * v:2 * v + 2, :], in_=vec.rearrange("(h p) -> h p", h=2))
         load_x(0, 0, 1)
         load_x(0, 1, 2)
         w_sb = const.tile([P, 2 * IN_F], BF16, name="w_sb")
@@ -85,10 +89,6 @@ def tile_modelnew_t_kernel(
 
         ident = const.tile([P, P], F32, name="ident")
         make_identity(nc, ident[:])
-        vrows = const.tile([P, P], BF16, name="vrows")
-        nc.gpsimd.memset(vrows[:], 0.0)
-        for v, vec in enumerate((bias, running_mean, running_var, norm_weight, norm_bias)):
-            nc.scalar.dma_start(out=vrows[2 * v:2 * v + 2, :], in_=vec.rearrange("(h p) -> h p", h=2))
         identb = const.tile([P, P], BF16, name="identb")
         make_identity(nc, identb[:])
         half = const.tile([P, 2], F32, name="half")
@@ -157,12 +157,13 @@ def tile_modelnew_t_kernel(
             return i % 4 != 1
 
         def stage_y(i):
-            nb = nbp.tile([P, JU * OUT_F], F32, name="nb", tag="nb")
             if y_on_pe(i):
-                nc.tensor.matmul(out=nb[:], lhsT=identb[:], rhs=y_cols(i), start=True, stop=False)
-            nbs[i] = nb
+                nbs[i] = nbp.tile([P, JU * OUT_F], F32, name="nb", tag="nb")
+                nc.tensor.matmul(out=nbs[i][:], lhsT=identb[:], rhs=y_cols(i), start=True, stop=False)
 
         def stage_b(i):
+            if not y_on_pe(i):
+                nbs[i] = nbp.tile([P, JU * OUT_F], F32, name="nb", tag="nb")
             add_y = y_on_pe(i)
             for jj in range(JU):
                 for h in range(2):
@@ -194,60 +195,68 @@ def tile_modelnew_t_kernel(
                 in_=outs[i // 2][:, (i % 2) * w:(i % 2 + n) * w],
             )
 
-        stage_r(0)
-        stage_r(1)
-        stage_x(0)
-        w32 = w_sb[:].bitcast(F32).rearrange("p (h w) -> p h w", h=2)
-        wgrp = const.tile([P, 2048], BF16, name="wgrp", align_bytes=64)
-        wgrp32 = wgrp[:].bitcast(F32).rearrange("p (g c u) -> p g c u", g=2, u=2)
-        for g in range(2):
-            wt = xtp.tile([P, 2, 256], F32, name="wt", tag="xt")
-            for u in range(2):
-                for h in range(2):
-                    nc.tensor.transpose(wt[:, u, h * P:(h + 1) * P], w32[:, h, 256 * g + u:256 * (g + 1):2], ident[:])
-            nc.scalar.copy(out=wgrp32[:, g], in_=wt[:].rearrange("p u c -> p c u"))
-        stage_q(0)
         wcod = const.tile([P, 512], U32, name="wcod", align_bytes=64)
         wscl = const.tile([P, 512], U8, name="wscl", align_bytes=64)
-        nc.vector.quantize_mx(out=wcod[:].bitcast(FP8X4), scales=wscl[:], in_=wgrp[:])
-
-        pv = nbp.tile([P, P], F32, name="pv", tag="nb")
-        nc.tensor.transpose(pv[:], vrows32[:], ident[:])
-        prm = const.tile([P, 10], F32, name="prm")
-        nc.scalar.copy(out=prm[:], in_=pv[:, 0:10])
-        tmp = const.tile([P, 8], F32, name="tmp")
         s_col = const.tile([P, 2], F32, name="s_col")
         t_col = const.tile([P, 2], F32, name="t_col")
-        nc.gpsimd.tensor_scalar(out=tmp[:, 0:2], in0=prm[:, 4:6], scalar1=EPS, scalar2=None, op0=ALU.add)
-        nc.gpsimd.tensor_tensor(out=tmp[:, 2:4], in0=tmp[:, 0:2], in1=half[:], op=ALU.pow)
-        nc.gpsimd.tensor_tensor(out=s_col[:], in0=tmp[:, 2:4], in1=prm[:, 6:8], op=ALU.mult)
-        nc.gpsimd.tensor_tensor(out=tmp[:, 4:6], in0=prm[:, 0:2], in1=prm[:, 2:4], op=ALU.subtract)
-        nc.gpsimd.tensor_tensor(out=tmp[:, 6:8], in0=tmp[:, 4:6], in1=s_col[:], op=ALU.mult)
-        nc.gpsimd.tensor_tensor(out=t_col[:], in0=tmp[:, 6:8], in1=prm[:, 8:10], op=ALU.add)
 
-        for k in range(NU + 2):
-            if 1 <= k < NU:
+        def weights_and_params():
+            w32 = w_sb[:].bitcast(F32).rearrange("p (h w) -> p h w", h=2)
+            wgrp = const.tile([P, 2048], BF16, name="wgrp", align_bytes=64)
+            wgrp32 = wgrp[:].bitcast(F32).rearrange("p (g c u) -> p g c u", g=2, u=2)
+            for g in range(2):
+                wt = xtp.tile([P, 2, 256], F32, name="wt", tag="xt")
+                for u in range(2):
+                    for h in range(2):
+                        nc.tensor.transpose(
+                            wt[:, u, h * P:(h + 1) * P], w32[:, h, 256 * g + u:256 * (g + 1):2], ident[:]
+                        )
+                nc.scalar.copy(out=wgrp32[:, g], in_=wt[:].rearrange("p u c -> p c u"))
+            nc.vector.quantize_mx(out=wcod[:].bitcast(FP8X4), scales=wscl[:], in_=wgrp[:])
+
+            pv = nbp.tile([P, P], F32, name="pv", tag="nb")
+            nc.tensor.transpose(pv[:], vrows32[:], ident[:])
+            prm = const.tile([P, 10], F32, name="prm")
+            nc.scalar.copy(out=prm[:], in_=pv[:, 0:10])
+            tmp = const.tile([P, 8], F32, name="tmp")
+            nc.gpsimd.tensor_scalar(out=tmp[:, 0:2], in0=prm[:, 4:6], scalar1=EPS, scalar2=None, op0=ALU.add)
+            nc.gpsimd.tensor_tensor(out=tmp[:, 2:4], in0=tmp[:, 0:2], in1=half[:], op=ALU.pow)
+            nc.gpsimd.tensor_tensor(out=s_col[:], in0=tmp[:, 2:4], in1=prm[:, 6:8], op=ALU.mult)
+            nc.gpsimd.tensor_tensor(out=tmp[:, 4:6], in0=prm[:, 0:2], in1=prm[:, 2:4], op=ALU.subtract)
+            nc.gpsimd.tensor_tensor(out=tmp[:, 6:8], in0=tmp[:, 4:6], in1=s_col[:], op=ALU.mult)
+            nc.gpsimd.tensor_tensor(out=t_col[:], in0=tmp[:, 6:8], in1=prm[:, 8:10], op=ALU.add)
+
+        def live(i):
+            return 0 <= i < NU
+
+        for k in range(-3, NU + 5):
+            if live(k - 4):
+                stage_u(k - 4)
+            if live(k - 5) and not y_on_pe(k - 5):
+                stage_u2(k - 5)
+            if k - 5 in (NU - 2, NU - 1):
+                stage_st(k - 5, 1)
+            elif live(k - 6) and k % 2 == 0:
+                stage_st(k - 6, 2)
+            if live(k):
                 stage_q(k)
-            if k >= 2 and not y_on_pe(k - 2):
-                stage_u2(k - 2)
-            if k >= 2 and k - 2 >= NU - 2:
-                stage_st(k - 2, 1)
-            elif k >= 2 and k % 2 == 1:
-                stage_st(k - 3, 2)
-            if k + 2 < NU:
-                stage_r(k + 2)
-                g_new = (k + 2) // UG + XB
-                if (k + 2) % UG == UG - 1 and g_new < NG:
+            if live(k + 3):
+                stage_r(k + 3)
+                g_new = (k + 3) // UG + XB
+                if (k + 3) % UG == UG - 1 and g_new < NG:
                     load_x(g_new, 0, 4)
                     load_y(g_new - 1)
                     if g_new == NG - 1:
                         load_y(g_new)
-            if k + 1 < NU:
+            if live(k - 2):
+                stage_a(k - 2)
+            if live(k + 1):
                 stage_x(k + 1)
-            if 1 <= k <= NU:
-                stage_b(k - 1)
-                stage_u(k - 1)
-            if k < NU:
-                stage_m(k)
-                stage_y(k)
-                stage_a(k)
+            if k == -1:
+                weights_and_params()
+            if live(k - 3):
+                stage_b(k - 3)
+            if live(k - 1):
+                stage_m(k - 1)
+            if live(k - 2):
+                stage_y(k - 2)

@@ -77,9 +77,11 @@ def tile_modelnew_t_kernel(
             out=w_sb[:].rearrange("p (h k) -> p h k", h=2),
             in_=weight.rearrange("(h p) k -> p h k", p=P),
         )
-        load_x(0, 2, 4)
+        load_x(0, 2, 3)
+        load_x(0, 3, 4)
         load_y(0)
-        load_x(1, 0, 4)
+        load_x(1, 0, 2)
+        load_x(1, 2, 4)
         load_y(1)
         load_x(2, 0, 4)
         load_y(2)
@@ -102,8 +104,8 @@ def tile_modelnew_t_kernel(
             q = i % UG
             x32 = xs[i // UG][:].bitcast(F32)[:, q * w:(q + 1) * w]
             nc.vector.tensor_copy(
-                out=xr[:].bitcast(F32).rearrange("p (n u w) -> p n u w", n=2 * JU, u=2),
-                in_=x32.rearrange("p (n w u) -> p n u w", n=2 * JU, u=2),
+                out=xr[:].bitcast(F32).rearrange("p (n u w) -> p n w u", n=2 * JU, u=2),
+                in_=x32.rearrange("p (n w u) -> p n w u", n=2 * JU, u=2),
             )
             xrs[i] = xr
 

@@ -99,26 +99,28 @@ def tile_modelnew_t_kernel(
         nc.gpsimd.tensor_copy(out=vrows32[:], in_=vrows[:])
 
         def stage_r(i):
-            xr = work.tile([P, JU * IN_F], BF16, name="xr", tag="xr")
-            w = JU * IN_F // 2
-            q = i % UG
-            x32 = xs[i // UG][:].bitcast(F32)[:, q * w:(q + 1) * w]
+            xr = work.tile([P, IN_F], BF16, name="xr", tag="xr")
+            w = IN_F // 2
+            r = (i % UG) * JU + 1
+            x32 = xs[i // UG][:].bitcast(F32)[:, r * w:(r + 1) * w]
             nc.vector.tensor_copy(
-                out=xr[:].bitcast(F32).rearrange("p (n u w) -> p n w u", n=2 * JU, u=2),
-                in_=x32.rearrange("p (n w u) -> p n w u", n=2 * JU, u=2),
+                out=xr[:].bitcast(F32).rearrange("p (n u w) -> p n w u", n=2, u=2),
+                in_=x32.rearrange("p (n w u) -> p n w u", n=2, u=2),
             )
             xrs[i] = xr
 
         def stage_x(i):
             grps[i] = work.tile([P, 2 * CU * 4], BF16, name="grp", tag="grp", align_bytes=64)
-            x32 = xrs[i][:].bitcast(F32).rearrange("p (j w) -> p j w", j=JU)
+            xr32 = xrs[i][:].bitcast(F32)
+            r0 = (i % UG) * JU * IN_F // 2
+            x32 = xs[i // UG][:].bitcast(F32)[:, r0:r0 + IN_F // 2]
             grp32 = grps[i][:].bitcast(F32).rearrange("p (g c u) -> p g c u", g=2, u=2)
             for g in range(2):
                 bank = xtp.tile([P, 2, CU], F32, name="xt", tag="xt")
                 for u in range(2):
-                    for jj in range(JU):
-                        c0 = 256 * g + 128 * u
-                        nc.tensor.transpose(bank[:, u, jj * P:(jj + 1) * P], x32[:, jj, c0:c0 + P], ident[:])
+                    c0 = 256 * g + 128 * u
+                    nc.tensor.transpose(bank[:, u, 0:P], x32[:, 256 * g + u:256 * (g + 1):2], ident[:])
+                    nc.tensor.transpose(bank[:, u, P:2 * P], xr32[:, c0:c0 + P], ident[:])
                 nc.scalar.copy(out=grp32[:, g], in_=bank[:].rearrange("p u c -> p c u"))
 
         def stage_q(i):
@@ -244,16 +246,16 @@ def tile_modelnew_t_kernel(
                 stage_q(k)
             if live(k + 3):
                 stage_r(k + 3)
-                g_new = (k + 3) // UG + XB
-                if (k + 3) % UG == UG - 1 and g_new < NG:
-                    load_x(g_new, 0, 4)
-                    load_y(g_new - 1)
-                    if g_new == NG - 1:
-                        load_y(g_new)
             if live(k - 2):
                 stage_a(k - 2)
             if live(k + 1):
                 stage_x(k + 1)
+                g_new = (k + 1) // UG + XB
+                if (k + 1) % UG == UG - 1 and g_new < NG:
+                    load_x(g_new, 0, 4)
+                    load_y(g_new - 1)
+                    if g_new == NG - 1:
+                        load_y(g_new)
             if k == -1:
                 weights_and_params()
             if live(k - 3):

@@ -58,8 +58,7 @@ def tile_modelnew_t_kernel(
         def load_x(g, lo, hi):
             if lo == 0:
                 xs[g] = xin.tile([P, JG * IN_F], BF16, name="xs", tag="xs")
-            w = JU * IN_F
-            nc.sync.dma_start(out=xs[g][:, lo * w:hi * w], in_=xv[g][:, lo * w:hi * w])
+            nc.sync.dma_start(out=xs[g][:, lo * IN_F:hi * IN_F], in_=xv[g][:, lo * IN_F:hi * IN_F])
 
         def load_y(g):
             yt = yin.tile([P, JG * OUT_F], BF16, name="ys", tag="ys")
@@ -68,26 +67,27 @@ def tile_modelnew_t_kernel(
 
         vrows = const.tile([P, P], BF16, name="vrows")
         nc.vector.memset(vrows[:], 0.0)
-        for v, vec in enumerate((bias, running_mean, running_var, norm_weight, norm_bias)):
-            nc.scalar.dma_start(out=vrows[2 * v:2 * v + 2, :], in_=vec.rearrange("(h p) -> h p", h=2))
         load_x(0, 0, 1)
         load_x(0, 1, 2)
+        load_x(0, 2, 4)
+        for v, vec in enumerate((bias, running_mean, running_var, norm_weight, norm_bias)):
+            nc.sync.dma_start(out=vrows[2 * v:2 * v + 2, :], in_=vec.rearrange("(h p) -> h p", h=2))
         w_sb = const.tile([P, 2 * IN_F], BF16, name="w_sb")
         nc.sync.dma_start(
             out=w_sb[:].rearrange("p (h k) -> p h k", h=2),
             in_=weight.rearrange("(h p) k -> p h k", p=P),
         )
-        load_x(0, 2, 3)
-        load_x(0, 3, 4)
+        load_x(0, 4, 6)
+        load_x(0, 6, 8)
         load_y(0)
-        load_x(1, 0, 2)
-        load_x(1, 2, 4)
+        load_x(1, 0, 4)
+        load_x(1, 4, 8)
         load_y(1)
-        load_x(2, 0, 4)
+        load_x(2, 0, 8)
         load_y(2)
-        load_x(3, 0, 4)
+        load_x(3, 0, 8)
         load_y(3)
-        load_x(4, 0, 4)
+        load_x(4, 0, 8)
 
         ident = const.tile([P, P], F32, name="ident")
         make_identity(nc, ident[:])
@@ -109,19 +109,35 @@ def tile_modelnew_t_kernel(
             )
             xrs[i] = xr
 
+        def copy_on_vector(i):
+            return i % 4 == 1 or i == NU - 1
+
         def stage_x(i):
             grps[i] = work.tile([P, 2 * CU * 4], BF16, name="grp", tag="grp", align_bytes=64)
             xr32 = xrs[i][:].bitcast(F32)
             r0 = (i % UG) * JU * IN_F // 2
             x32 = xs[i // UG][:].bitcast(F32)[:, r0:r0 + IN_F // 2]
             grp32 = grps[i][:].bitcast(F32).rearrange("p (g c u) -> p g c u", g=2, u=2)
+            banks = [xtp.tile([P, 2, CU], F32, name="xt", tag="xt") for g in range(2)]
+
+            def turn(g, u, jj):
+                c0 = 256 * g + 128 * u
+                src = x32[:, 256 * g + u:256 * (g + 1):2] if jj == 0 else xr32[:, c0:c0 + P]
+                nc.tensor.transpose(banks[g][:, u, jj * P:(jj + 1) * P], src, ident[:])
+
+            if i == 0:
+                for jj in range(JU):
+                    for g in range(2):
+                        for u in range(2):
+                            turn(g, u, jj)
+            else:
+                for g in range(2):
+                    for u in range(2):
+                        for jj in range(JU):
+                            turn(g, u, jj)
             for g in range(2):
-                bank = xtp.tile([P, 2, CU], F32, name="xt", tag="xt")
-                for u in range(2):
-                    c0 = 256 * g + 128 * u
-                    nc.tensor.transpose(bank[:, u, 0:P], x32[:, 256 * g + u:256 * (g + 1):2], ident[:])
-                    nc.tensor.transpose(bank[:, u, P:2 * P], xr32[:, c0:c0 + P], ident[:])
-                nc.scalar.copy(out=grp32[:, g], in_=bank[:].rearrange("p u c -> p c u"))
+                copy = nc.vector.tensor_copy if g == 0 and copy_on_vector(i) else nc.scalar.copy
+                copy(out=grp32[:, g], in_=banks[g][:].rearrange("p u c -> p c u"))
 
         def stage_q(i):
             cods[i] = work.tile([P, 2 * CU], U32, name="cod", tag="cod", align_bytes=64)
@@ -204,7 +220,7 @@ def tile_modelnew_t_kernel(
         s_col = const.tile([P, 2], F32, name="s_col")
         t_col = const.tile([P, 2], F32, name="t_col")
 
-        def weights_and_params():
+        def weights():
             w32 = w_sb[:].bitcast(F32).rearrange("p (h w) -> p h w", h=2)
             wgrp = const.tile([P, 2048], BF16, name="wgrp", align_bytes=64)
             wgrp32 = wgrp[:].bitcast(F32).rearrange("p (g c u) -> p g c u", g=2, u=2)
@@ -215,9 +231,10 @@ def tile_modelnew_t_kernel(
                         nc.tensor.transpose(
                             wt[:, u, h * P:(h + 1) * P], w32[:, h, 256 * g + u:256 * (g + 1):2], ident[:]
                         )
-                nc.scalar.copy(out=wgrp32[:, g], in_=wt[:].rearrange("p u c -> p c u"))
+                nc.vector.tensor_copy(out=wgrp32[:, g], in_=wt[:].rearrange("p u c -> p c u"))
             nc.vector.quantize_mx(out=wcod[:].bitcast(FP8X4), scales=wscl[:], in_=wgrp[:])
 
+        def params():
             pv = nbp.tile([P, P], F32, name="pv", tag="nb")
             nc.tensor.transpose(pv[:], vrows32[:], ident[:])
             prm = const.tile([P, 10], F32, name="prm")
@@ -233,7 +250,7 @@ def tile_modelnew_t_kernel(
         def live(i):
             return 0 <= i < NU
 
-        for k in range(-3, NU + 5):
+        for k in range(-2, NU + 5):
             if live(k - 4):
                 stage_u(k - 4)
             if live(k - 5) and not y_on_pe(k - 5):
@@ -244,20 +261,21 @@ def tile_modelnew_t_kernel(
                 stage_st(k - 6, 2)
             if live(k):
                 stage_q(k)
-            if live(k + 3):
-                stage_r(k + 3)
+            if live(k + 2):
+                stage_r(k + 2)
             if live(k - 2):
                 stage_a(k - 2)
             if live(k + 1):
                 stage_x(k + 1)
                 g_new = (k + 1) // UG + XB
                 if (k + 1) % UG == UG - 1 and g_new < NG:
-                    load_x(g_new, 0, 4)
+                    load_x(g_new, 0, JG)
                     load_y(g_new - 1)
                     if g_new == NG - 1:
                         load_y(g_new)
-            if k == -1:
-                weights_and_params()
+            if k == 0:
+                params()
+                weights()
             if live(k - 3):
                 stage_b(k - 3)
             if live(k - 1):

@@ -48,6 +48,7 @@ def tile_modelnew_t_kernel(
         ys = {}
         xrs = {}
         grps = {}
+        late = {}
         cods = {}
         scls = {}
         lins = {}
@@ -69,23 +70,25 @@ def tile_modelnew_t_kernel(
         nc.vector.memset(vrows[:], 0.0)
         load_x(0, 0, 1)
         load_x(0, 1, 2)
-        load_x(0, 2, 4)
-        for v, vec in enumerate((bias, running_mean, running_var, norm_weight, norm_bias)):
-            nc.sync.dma_start(out=vrows[2 * v:2 * v + 2, :], in_=vec.rearrange("(h p) -> h p", h=2))
         w_sb = const.tile([P, 2 * IN_F], BF16, name="w_sb")
         nc.sync.dma_start(
             out=w_sb[:].rearrange("p (h k) -> p h k", h=2),
             in_=weight.rearrange("(h p) k -> p h k", p=P),
         )
+        for v, vec in enumerate((bias, running_mean, running_var, norm_weight, norm_bias)):
+            nc.sync.dma_start(out=vrows[2 * v:2 * v + 2, :], in_=vec.rearrange("(h p) -> h p", h=2))
+        load_x(0, 2, 4)
         load_x(0, 4, 6)
         load_x(0, 6, 8)
         load_y(0)
         load_x(1, 0, 4)
         load_x(1, 4, 8)
         load_y(1)
-        load_x(2, 0, 8)
+        load_x(2, 0, 4)
+        load_x(2, 4, 8)
         load_y(2)
-        load_x(3, 0, 8)
+        load_x(3, 0, 4)
+        load_x(3, 4, 8)
         load_y(3)
         load_x(4, 0, 8)
 
@@ -97,6 +100,9 @@ def tile_modelnew_t_kernel(
         nc.gpsimd.memset(half[:], -0.5)
         vrows32 = const.tile([P, P], F32, name="vrows32")
         nc.gpsimd.tensor_copy(out=vrows32[:], in_=vrows[:])
+
+        def reordered(i, jj):
+            return jj == 1 and i >= 3
 
         def stage_r(i):
             xr = work.tile([P, IN_F], BF16, name="xr", tag="xr")
@@ -110,34 +116,29 @@ def tile_modelnew_t_kernel(
             xrs[i] = xr
 
         def copy_on_vector(i):
-            return i % 4 == 1 or i == NU - 1
+            return i % 10 == 5 or i == NU - 1
 
         def stage_x(i):
             grps[i] = work.tile([P, 2 * CU * 4], BF16, name="grp", tag="grp", align_bytes=64)
-            xr32 = xrs[i][:].bitcast(F32)
-            r0 = (i % UG) * JU * IN_F // 2
-            x32 = xs[i // UG][:].bitcast(F32)[:, r0:r0 + IN_F // 2]
+            w = IN_F // 2
+            r0 = (i % UG) * JU * w
+            x32 = xs[i // UG][:].bitcast(F32)[:, r0:r0 + JU * w].rearrange("p (j w) -> p j w", j=JU)
             grp32 = grps[i][:].bitcast(F32).rearrange("p (g c u) -> p g c u", g=2, u=2)
-            banks = [xtp.tile([P, 2, CU], F32, name="xt", tag="xt") for g in range(2)]
-
-            def turn(g, u, jj):
-                c0 = 256 * g + 128 * u
-                src = x32[:, 256 * g + u:256 * (g + 1):2] if jj == 0 else xr32[:, c0:c0 + P]
-                nc.tensor.transpose(banks[g][:, u, jj * P:(jj + 1) * P], src, ident[:])
-
-            if i == 0:
-                for jj in range(JU):
-                    for g in range(2):
-                        for u in range(2):
-                            turn(g, u, jj)
-            else:
-                for g in range(2):
-                    for u in range(2):
-                        for jj in range(JU):
-                            turn(g, u, jj)
             for g in range(2):
-                copy = nc.vector.tensor_copy if g == 0 and copy_on_vector(i) else nc.scalar.copy
-                copy(out=grp32[:, g], in_=banks[g][:].rearrange("p u c -> p c u"))
+                bank = xtp.tile([P, 2, CU], F32, name="xt", tag="xt")
+                for jj in range(JU):
+                    for u in range(2):
+                        if reordered(i, jj):
+                            c0 = 256 * g + 128 * u
+                            src = xrs[i][:].bitcast(F32)[:, c0:c0 + P]
+                        else:
+                            src = x32[:, jj, 256 * g + u:256 * (g + 1):2]
+                        nc.tensor.transpose(bank[:, u, jj * P:(jj + 1) * P], src, ident[:])
+                src = bank[:].rearrange("p u c -> p c u")
+                if g == 0 and copy_on_vector(i):
+                    late[i] = (grp32[:, g], src)
+                else:
+                    nc.scalar.copy(out=grp32[:, g], in_=src)
 
         def stage_q(i):
             cods[i] = work.tile([P, 2 * CU], U32, name="cod", tag="cod", align_bytes=64)
@@ -174,7 +175,7 @@ def tile_modelnew_t_kernel(
             return ys[i // UG][:, q * JU * OUT_F:(q + 1) * JU * OUT_F]
 
         def y_on_pe(i):
-            return i % 4 != 1
+            return i % 5 != 1
 
         def stage_y(i):
             if y_on_pe(i):
@@ -231,7 +232,8 @@ def tile_modelnew_t_kernel(
                         nc.tensor.transpose(
                             wt[:, u, h * P:(h + 1) * P], w32[:, h, 256 * g + u:256 * (g + 1):2], ident[:]
                         )
-                nc.vector.tensor_copy(out=wgrp32[:, g], in_=wt[:].rearrange("p u c -> p c u"))
+                copy = nc.scalar.copy if g == 0 else nc.vector.tensor_copy
+                copy(out=wgrp32[:, g], in_=wt[:].rearrange("p u c -> p c u"))
             nc.vector.quantize_mx(out=wcod[:].bitcast(FP8X4), scales=wscl[:], in_=wgrp[:])
 
         def params():
@@ -250,7 +252,9 @@ def tile_modelnew_t_kernel(
         def live(i):
             return 0 <= i < NU
 
-        for k in range(-2, NU + 5):
+        for k in range(-1, NU + 5):
+            if k in late:
+                nc.vector.tensor_copy(out=late[k][0], in_=late[k][1])
             if live(k - 4):
                 stage_u(k - 4)
             if live(k - 5) and not y_on_pe(k - 5):
@@ -261,8 +265,8 @@ def tile_modelnew_t_kernel(
                 stage_st(k - 6, 2)
             if live(k):
                 stage_q(k)
-            if live(k + 2):
-                stage_r(k + 2)
+            if live(k + 3) and reordered(k + 3, 1):
+                stage_r(k + 3)
             if live(k - 2):
                 stage_a(k - 2)
             if live(k + 1):
@@ -273,9 +277,9 @@ def tile_modelnew_t_kernel(
                     load_y(g_new - 1)
                     if g_new == NG - 1:
                         load_y(g_new)
-            if k == 0:
-                params()
+            if k == -1:
                 weights()
+                params()
             if live(k - 3):
                 stage_b(k - 3)
             if live(k - 1):

from contextlib import ExitStack

import concourse.mybir as mybir
from concourse.masks import make_identity

F32 = mybir.dt.float32
BF16 = mybir.dt.bfloat16
U32 = mybir.dt.uint32
U8 = mybir.dt.uint8
FP8X4 = mybir.dt.float8_e4m3fn_x4
ACT = mybir.ActivationFunctionType
ALU = mybir.AluOpType

P = 128
B, IN_F, OUT_F = 10240, 1024, 256
EPS = 1e-5
FLOPS = 2 * B * IN_F * OUT_F

JG = 8
NG = B // (P * JG)
JU = 2
CU = JU * P
UG = JG // JU
NU = B // CU
XB = 5


def tile_modelnew_t_kernel(
    tc, x, y, weight, bias, running_mean, running_var, norm_weight, norm_bias, out
):
    nc = tc.nc
    xv = x.rearrange("(g p j) k -> g p (j k)", p=P, j=JG)
    yv = y.rearrange("(g p j) f -> g p (j f)", p=P, j=JG)
    ov = out.rearrange("(g p j) f -> g p (j f)", p=P, j=JG)

    with ExitStack() as ctx:
        ctx.enter_context(tc.manual_schedule())
        const = ctx.enter_context(tc.tile_pool(name="const", bufs=1))
        xin = ctx.enter_context(tc.tile_pool(name="xin", bufs=XB))
        yin = ctx.enter_context(tc.tile_pool(name="yin", bufs=6))
        work = ctx.enter_context(tc.tile_pool(name="work", bufs=4))
        outp = ctx.enter_context(tc.tile_pool(name="outp", bufs=8))
        xtp = ctx.enter_context(tc.psum_pool(name="xtp", bufs=4))
        linp = ctx.enter_context(tc.psum_pool(name="linp", bufs=2))
        nbp = ctx.enter_context(tc.psum_pool(name="nbp", bufs=2))

        xs = {}
        ys = {}
        xrs = {}
        grps = {}
        late = {}
        cods = {}
        scls = {}
        lins = {}
        nts = {}
        nbs = {}
        outs = {}

        def load_x(g, lo, hi):
            if lo == 0:
                xs[g] = xin.tile([P, JG * IN_F], BF16, name="xs", tag="xs")
            nc.sync.dma_start(out=xs[g][:, lo * IN_F:hi * IN_F], in_=xv[g][:, lo * IN_F:hi * IN_F])

        def load_y(g):
            yt = yin.tile([P, JG * OUT_F], BF16, name="ys", tag="ys")
            nc.sync.dma_start(out=yt[:], in_=yv[g])
            ys[g] = yt

        vrows = const.tile([P, P], BF16, name="vrows")
        nc.vector.memset(vrows[:], 0.0)
        load_x(0, 0, 1)
        load_x(0, 1, 2)
        w_sb = const.tile([P, 2 * IN_F], BF16, name="w_sb")
        nc.sync.dma_start(
            out=w_sb[:].rearrange("p (h k) -> p h k", h=2),
            in_=weight.rearrange("(h p) k -> p h k", p=P),
        )
        for v, vec in enumerate((bias, running_mean, running_var, norm_weight, norm_bias)):
            nc.sync.dma_start(out=vrows[2 * v:2 * v + 2, :], in_=vec.rearrange("(h p) -> h p", h=2))
        load_x(0, 2, 4)
        load_x(0, 4, 6)
        load_x(0, 6, 8)
        load_y(0)
        load_x(1, 0, 4)
        load_x(1, 4, 8)
        load_y(1)
        load_x(2, 0, 4)
        load_x(2, 4, 8)
        load_y(2)
        load_x(3, 0, 4)
        load_x(3, 4, 8)
        load_y(3)
        load_x(4, 0, 8)

        ident = const.tile([P, P], F32, name="ident")
        make_identity(nc, ident[:])
        identb = const.tile([P, P], BF16, name="identb")
        make_identity(nc, identb[:])
        half = const.tile([P, 2], F32, name="half")
        nc.gpsimd.memset(half[:], -0.5)
        vrows32 = const.tile([P, P], F32, name="vrows32")
        nc.gpsimd.tensor_copy(out=vrows32[:], in_=vrows[:])

        def reordered(i, jj):
            return jj == 1 and i >= 3

        def stage_r(i):
            xr = work.tile([P, IN_F], BF16, name="xr", tag="xr")
            w = IN_F // 2
            r = (i % UG) * JU + 1
            x32 = xs[i // UG][:].bitcast(F32)[:, r * w:(r + 1) * w]
            nc.vector.tensor_copy(
                out=xr[:].bitcast(F32).rearrange("p (n u w) -> p n w u", n=2, u=2),
                in_=x32.rearrange("p (n w u) -> p n w u", n=2, u=2),
            )
            xrs[i] = xr

        def copy_on_vector(i):
            return i % 10 == 5 or i == NU - 1

        def stage_x(i):
            grps[i] = work.tile([P, 2 * CU * 4], BF16, name="grp", tag="grp", align_bytes=64)
            w = IN_F // 2
            r0 = (i % UG) * JU * w
            x32 = xs[i // UG][:].bitcast(F32)[:, r0:r0 + JU * w].rearrange("p (j w) -> p j w", j=JU)
            grp32 = grps[i][:].bitcast(F32).rearrange("p (g c u) -> p g c u", g=2, u=2)
            for g in range(2):
                bank = xtp.tile([P, 2, CU], F32, name="xt", tag="xt")
                for jj in range(JU):
                    for u in range(2):
                        if reordered(i, jj):
                            c0 = 256 * g + 128 * u
                            src = xrs[i][:].bitcast(F32)[:, c0:c0 + P]
                        else:
                            src = x32[:, jj, 256 * g + u:256 * (g + 1):2]
                        nc.tensor.transpose(bank[:, u, jj * P:(jj + 1) * P], src, ident[:])
                src = bank[:].rearrange("p u c -> p c u")
                if g == 0 and copy_on_vector(i):
                    late[i] = (grp32[:, g], src)
                else:
                    nc.scalar.copy(out=grp32[:, g], in_=src)

        def stage_q(i):
            cods[i] = work.tile([P, 2 * CU], U32, name="cod", tag="cod", align_bytes=64)
            scls[i] = work.tile([P, 2 * CU], U8, name="scl", tag="scl", align_bytes=64)
            nc.vector.quantize_mx(out=cods[i][:].bitcast(FP8X4), scales=scls[i][:], in_=grps[i][:])

        def stage_m(i):
            lin = linp.tile([P, 2, CU], F32, name="lin", tag="lin")
            for h in range(2):
                for g in range(2):
                    w0 = g * 256 + h * P
                    nc.tensor.matmul_mx(
                        out=lin[:, h, :],
                        lhsT=wcod[:, w0:w0 + P].bitcast(FP8X4),
                        lhsT_scale=wscl[:, w0:w0 + P],
                        rhs=cods[i][:, g * CU:(g + 1) * CU].bitcast(FP8X4),
                        rhs_scale=scls[i][:, g * CU:(g + 1) * CU],
                        start=(g == 0),
                        stop=(g == 1),
                    )
            lins[i] = lin

        def stage_a(i):
            nt = work.tile([P, 2, CU], F32, name="nt", tag="nt")
            for h in range(2):
                nc.scalar.activation(
                    out=nt[:, h, :], in_=lins[i][:, h, :], func=ACT.Identity,
                    scale=s_col[:, h:h + 1], bias=t_col[:, h:h + 1],
                )
            nts[i] = nt

        def y_cols(i):
            q = i % UG
            return ys[i // UG][:, q * JU * OUT_F:(q + 1) * JU * OUT_F]

        def y_on_pe(i):
            return i % 5 != 1

        def stage_y(i):
            if y_on_pe(i):
                nbs[i] = nbp.tile([P, JU * OUT_F], F32, name="nb", tag="nb")
                nc.tensor.matmul(out=nbs[i][:], lhsT=identb[:], rhs=y_cols(i), start=True, stop=False)

        def stage_b(i):
            if not y_on_pe(i):
                nbs[i] = nbp.tile([P, JU * OUT_F], F32, name="nb", tag="nb")
            add_y = y_on_pe(i)
            for jj in range(JU):
                for h in range(2):
                    c0 = jj * OUT_F + h * P
                    nc.tensor.matmul(
                        out=nbs[i][:, c0:c0 + P], lhsT=nts[i][:, h, jj * P:(jj + 1) * P], rhs=ident[:],
                        start=not add_y, stop=(not add_y) or (jj == 1 and h == 1), is_transpose=True,
                    )

        def o_cols(i):
            if i % 2 == 0:
                outs[i // 2] = outp.tile([P, 2 * JU * OUT_F], F32, name="o", tag="o")
            w = JU * OUT_F
            return outs[i // 2][:, (i % 2) * w:(i % 2 + 1) * w]

        def stage_u(i):
            op = ALU.mult if y_on_pe(i) else ALU.add
            nc.vector.tensor_tensor(out=o_cols(i), in0=nbs[i][:], in1=y_cols(i), op=op)

        def stage_u2(i):
            w = JU * OUT_F
            o = outs[i // 2][:, (i % 2) * w:(i % 2 + 1) * w]
            nc.vector.tensor_tensor(out=o, in0=o, in1=y_cols(i), op=ALU.mult)

        def stage_st(i, n):
            w = JU * OUT_F
            nc.sync.dma_start(
                out=ov[i // UG][:, (i % UG) * w:(i % UG + n) * w],
                in_=outs[i // 2][:, (i % 2) * w:(i % 2 + n) * w],
            )

        wcod = const.tile([P, 512], U32, name="wcod", align_bytes=64)
        wscl = const.tile([P, 512], U8, name="wscl", align_bytes=64)
        s_col = const.tile([P, 2], F32, name="s_col")
        t_col = const.tile([P, 2], F32, name="t_col")

        def weights():
            w32 = w_sb[:].bitcast(F32).rearrange("p (h w) -> p h w", h=2)
            wgrp = const.tile([P, 2048], BF16, name="wgrp", align_bytes=64)
            wgrp32 = wgrp[:].bitcast(F32).rearrange("p (g c u) -> p g c u", g=2, u=2)
            for g in range(2):
                wt = xtp.tile([P, 2, 256], F32, name="wt", tag="xt")
                for u in range(2):
                    for h in range(2):
                        nc.tensor.transpose(
                            wt[:, u, h * P:(h + 1) * P], w32[:, h, 256 * g + u:256 * (g + 1):2], ident[:]
                        )
                copy = nc.scalar.copy if g == 0 else nc.vector.tensor_copy
                copy(out=wgrp32[:, g], in_=wt[:].rearrange("p u c -> p c u"))
            nc.vector.quantize_mx(out=wcod[:].bitcast(FP8X4), scales=wscl[:], in_=wgrp[:])

        def params():
            pv = nbp.tile([P, P], F32, name="pv", tag="nb")
            nc.tensor.transpose(pv[:], vrows32[:], ident[:])
            prm = const.tile([P, 10], F32, name="prm")
            nc.scalar.copy(out=prm[:], in_=pv[:, 0:10])
            tmp = const.tile([P, 8], F32, name="tmp")
            nc.gpsimd.tensor_scalar(out=tmp[:, 0:2], in0=prm[:, 4:6], scalar1=EPS, scalar2=None, op0=ALU.add)
            nc.gpsimd.tensor_tensor(out=tmp[:, 2:4], in0=tmp[:, 0:2], in1=half[:], op=ALU.pow)
            nc.gpsimd.tensor_tensor(out=s_col[:], in0=tmp[:, 2:4], in1=prm[:, 6:8], op=ALU.mult)
            nc.gpsimd.tensor_tensor(out=tmp[:, 4:6], in0=prm[:, 0:2], in1=prm[:, 2:4], op=ALU.subtract)
            nc.gpsimd.tensor_tensor(out=tmp[:, 6:8], in0=tmp[:, 4:6], in1=s_col[:], op=ALU.mult)
            nc.gpsimd.tensor_tensor(out=t_col[:], in0=tmp[:, 6:8], in1=prm[:, 8:10], op=ALU.add)

        def live(i):
            return 0 <= i < NU

        for k in range(-1, NU + 5):
            if k in late:
                nc.vector.tensor_copy(out=late[k][0], in_=late[k][1])
            if live(k - 4):
                stage_u(k - 4)
            if live(k - 5) and not y_on_pe(k - 5):
                stage_u2(k - 5)
            if k - 5 in (NU - 2, NU - 1):
                stage_st(k - 5, 1)
            elif live(k - 6) and k % 2 == 0:
                stage_st(k - 6, 2)
            if live(k):
                stage_q(k)
            if live(k + 3) and reordered(k + 3, 1):
                stage_r(k + 3)
            if live(k - 2):
                stage_a(k - 2)
            if live(k + 1):
                stage_x(k + 1)
                g_new = (k + 1) // UG + XB
                if (k + 1) % UG == UG - 1 and g_new < NG:
                    load_x(g_new, 0, JG)
                    load_y(g_new - 1)
                    if g_new == NG - 1:
                        load_y(g_new)
            if k == -1:
                weights()
                params()
            if live(k - 3):
                stage_b(k - 3)
            if live(k - 1):
                stage_m(k - 1)
            if live(k - 2):
                stage_y(k - 2)
